import numpy as np
import ml_dtypes


def mxq(x, axis, fmt="e4m3"):
    dtype, down = {"e4m3": (ml_dtypes.float8_e4m3fn, 7), "e5m2": (ml_dtypes.float8_e5m2, 14)}[fmt]
    v = np.moveaxis(np.asarray(x, np.float32).astype(ml_dtypes.bfloat16).astype(np.float64), axis, -1)
    blocks = v.reshape(v.shape[:-1] + (-1, 32))
    amax = np.abs(blocks).max(-1, keepdims=True)
    byte = np.maximum(np.where(amax > 0, np.frexp(amax)[1] - 1 + 127, 0) - down, 1)
    scale = np.exp2(byte - 127.0)
    codes = (blocks / scale).astype(np.float32).astype(dtype).astype(np.float64)
    return np.moveaxis((codes * scale).reshape(v.shape), -1, axis)


WIDE = False


def mx_kscale(k):
    if not WIDE:
        return np.ones(k)
    levels = np.array([10, -10, 5, -5, 0])
    a = np.random.permutation(np.resize(levels, k // 512 * 4)).reshape(k // 512, 4)
    idx = np.arange(k)
    return np.exp2(a[idx // 512, idx % 128 // 32])


BF16 = ml_dtypes.bfloat16


def bf(x):
    return np.asarray(x, np.float32).astype(BF16)


def f64(x):
    return np.asarray(x).astype(np.float64)


B, S, H, NH = 16, 256, 512, 8
DK = H // NH
NORM_EPS = 1e-6


def elu(v):
    return np.where(v > 0.0, v, np.exp(np.minimum(v, 0.0)) - 1.0)


def setup_inputs():
    s = mx_kscale(H)
    w = 1.0 / np.sqrt(H)
    return {"hidden_states": bf(np.random.standard_normal((B, S, H)) * s),
            "Wq": bf(np.random.standard_normal((H, H)) * 1.5 * w / s[:, None]),
            "Wk": bf(np.random.standard_normal((H, H)) * 1.5 * w / s[:, None]),
            "Wv": bf(np.random.standard_normal((H, H)) * 2.0 * w / s[:, None])}


def reference(hidden_states, Wq, Wk, Wv):
    xq = mxq(f64(hidden_states), 2, "e4m3")
    q = (xq @ mxq(f64(Wq), 0, "e4m3")).reshape(B, S, NH, DK)
    k = (xq @ mxq(f64(Wk), 0, "e4m3")).reshape(B, S, NH, DK)
    v = (xq @ mxq(f64(Wv), 0, "e4m3")).reshape(B, S, NH, DK)
    q = elu(q) + 1.0
    k = elu(k) + 1.0
    qk = np.sum(q * k, axis=-1, keepdims=True)
    k_sum = np.sum(k, axis=1, keepdims=True)
    normalizer = np.sum(q * k_sum, axis=-1, keepdims=True)
    z = qk * v / (normalizer + NORM_EPS)
    return z.reshape(B, S, H)

@@ -1,0 +1,276 @@
+from contextlib import ExitStack
+
+import concourse.mybir as mybir
+from concourse.masks import make_identity
+
+F32 = mybir.dt.float32
+BF16 = mybir.dt.bfloat16
+U32 = mybir.dt.uint32
+U8 = mybir.dt.uint8
+FP8X4 = mybir.dt.float8_e4m3fn_x4
+ALU = mybir.AluOpType
+ACT = mybir.ActivationFunctionType
+
+P = 128
+PACK = 4
+BATCHES, TOKENS, HIDDEN, HEADS = 16, 256, 512, 8
+HEAD_DIM = HIDDEN // HEADS
+NORM_EPS = 1e-6
+
+GROUP_BATCHES = 2
+GROUP_TOKENS = GROUP_BATCHES * TOKENS
+GROUPS = BATCHES // GROUP_BATCHES
+TILES = GROUP_TOKENS // P
+BATCH_TILES = TOKENS // P
+FEATURE_BLOCKS = HIDDEN // P
+BLOCK_HEADS = P // HEAD_DIM
+UNITS = GROUPS * FEATURE_BLOCKS
+
+SUMS_LAG = 2
+VALUE_LAG = FEATURE_BLOCKS - 1 + SUMS_LAG
+
+FLOPS = 3 * 2 * BATCHES * TOKENS * HIDDEN * HIDDEN
+
+
+def tile_gatedlinearattention_pa_t_kernel(tc, hidden_states, Wq, Wk, Wv, out):
+    nc = tc.nc
+    with ExitStack() as stack:
+        keep = stack.enter_context(tc.tile_pool(name="keep", bufs=1))
+        stage = stack.enter_context(tc.tile_pool(name="stage", bufs=2))
+        work = stack.enter_context(tc.tile_pool(name="work", bufs=3))
+        lagged = stack.enter_context(tc.tile_pool(name="lagged", bufs=SUMS_LAG + 2))
+        proj_psum = stack.enter_context(tc.psum_pool(name="proj_psum", bufs=4))
+        aux_psum = stack.enter_context(tc.psum_pool(name="aux_psum", bufs=3))
+        sums_psum = stack.enter_context(tc.psum_pool(name="sums_psum", bufs=1))
+        stack.enter_context(tc.manual_schedule())
+
+        x_raw = keep.tile([P, GROUPS, GROUP_TOKENS * HIDDEN // P], BF16)
+
+        def load_x(g):
+            batches = hidden_states[GROUP_BATCHES * g : GROUP_BATCHES * (g + 1)]
+            nc.sync.dma_start(
+                out=x_raw[:, g, :].rearrange("r (b w) -> r b w", b=GROUP_BATCHES),
+                in_=batches.rearrange("b (r j) k -> r b (j k)", j=BATCH_TILES),
+            )
+
+        def load_weight(w, raw):
+            nc.sync.dma_start(
+                out=raw[:].rearrange("p (u w) -> p u w", u=2),
+                in_=w.rearrange("(u p e) n -> p u (e n)", u=2, e=2),
+            )
+
+        wq_raw = keep.tile([P, PACK * HIDDEN], BF16)
+        wk_raw = keep.tile([P, PACK * HIDDEN], BF16)
+        wv_raw = keep.tile([P, PACK * HIDDEN], BF16)
+        load_x(0)
+        load_weight(Wk, wk_raw)
+        load_weight(Wq, wq_raw)
+        load_weight(Wv, wv_raw)
+        for g in range(1, GROUPS):
+            load_x(g)
+
+        identity = keep.tile([P, P], F32)
+        make_identity(nc, identity[:])
+        head_of_row = keep.tile([P, BLOCK_HEADS], F32)
+        nc.vector.memset(head_of_row[:], 0.0)
+        for h in range(BLOCK_HEADS):
+            nc.vector.memset(head_of_row[h * HEAD_DIM : (h + 1) * HEAD_DIM, h : h + 1], 1.0)
+        table_warmer = keep.tile([P, 1], F32)
+        nc.vector.memset(table_warmer[:], 0.0)
+        nc.scalar.activation(out=table_warmer[:], in_=table_warmer[:], func=ACT.Exp)
+
+        def regroup_weight(raw, grouped):
+            nc.vector.tensor_copy(
+                out=grouped[:].rearrange("p (c i t) -> p c t i", i=4, t=PACK),
+                in_=raw[:].rearrange("p (t c i) -> p c t i", t=PACK, i=4),
+            )
+
+        def quantise(grouped, codes, scales):
+            nc.vector.quantize_mx(out=codes.bitcast(FP8X4), scales=scales, in_=grouped[:])
+
+        wq_grouped = keep.tile([P, HIDDEN * PACK], BF16, align_bytes=64)
+        wk_grouped = keep.tile([P, HIDDEN * PACK], BF16, align_bytes=64)
+        wv_grouped = keep.tile([P, HIDDEN * PACK], BF16, align_bytes=64)
+        wq_codes = keep.tile([P, HIDDEN], U32, align_bytes=64)
+        wk_codes = keep.tile([P, HIDDEN], U32, align_bytes=64)
+        wv_codes = keep.tile([P, HIDDEN], U32, align_bytes=64)
+        wq_scales = keep.tile([P, HIDDEN], U8, align_bytes=64)
+        wk_scales = keep.tile([P, HIDDEN], U8, align_bytes=64)
+        wv_scales = keep.tile([P, HIDDEN], U8, align_bytes=64)
+        x_codes = keep.tile([P, GROUPS * GROUP_TOKENS], U32, align_bytes=64)
+        x_scales = keep.tile([P, GROUPS * GROUP_TOKENS], U8, align_bytes=64)
+
+        def prepare_x(g):
+            words = x_raw[:, g, :].bitcast(F32)
+            token_words = HIDDEN // 2
+            x_grouped = stage.tile([P, GROUP_TOKENS * PACK], BF16, align_bytes=64)
+            grouped_words = x_grouped[:].bitcast(F32)
+            for b in range(GROUP_BATCHES):
+                xt = aux_psum.tile([P, 2, TOKENS], F32, tag="aux")
+                for j in range(BATCH_TILES):
+                    for u in range(2):
+                        first = (b * BATCH_TILES + j) * token_words + u * P
+                        nc.tensor.transpose(
+                            xt[:, u, j * P : (j + 1) * P], words[:, first : first + P], identity[:]
+                        )
+                nc.scalar.copy(
+                    out=grouped_words[:, b * 2 * TOKENS : (b + 1) * 2 * TOKENS].rearrange(
+                        "p (c u) -> p c u", u=2
+                    ),
+                    in_=xt[:].rearrange("p u c -> p c u"),
+                )
+            tokens = slice(g * GROUP_TOKENS, (g + 1) * GROUP_TOKENS)
+            quantise(x_grouped, x_codes[:, tokens], x_scales[:, tokens])
+
+        live = {}
+
+        def project(s):
+            g, block = divmod(s, FEATURE_BLOCKS)
+            tokens = slice(g * GROUP_TOKENS, (g + 1) * GROUP_TOKENS)
+            features = slice(block * P, (block + 1) * P)
+            for name, codes, scales in (("c", wk_codes, wk_scales), ("a", wq_codes, wq_scales)):
+                acc = proj_psum.tile([P, GROUP_TOKENS], F32, tag="proj", name="acc_" + name)
+                nc.tensor.matmul_mx(
+                    out=acc[:],
+                    lhsT=codes[:, features].bitcast(FP8X4),
+                    lhsT_scale=scales[:, features],
+                    rhs=x_codes[:, tokens].bitcast(FP8X4),
+                    rhs_scale=x_scales[:, tokens],
+                    start=True,
+                    stop=True,
+                )
+                live[(name, s)] = acc
+            for name in ("c", "a"):
+                grown = work.tile([P, GROUP_TOKENS], F32, name="exp_" + name)
+                nc.scalar.activation(out=grown[:], in_=live[(name, s)][:], func=ACT.Exp)
+                capped = work.tile([P, GROUP_TOKENS], F32, name="capped_" + name)
+                nc.gpsimd.tensor_scalar(
+                    out=capped[:], in0=grown[:], scalar1=1.0, scalar2=0.0, op0=ALU.min, op1=ALU.max
+                )
+                live[("capped_" + name, s)] = capped
+
+        def combine(s):
+            k = work.tile([P, GROUP_TOKENS], F32)
+            k_sum = lagged.tile([P, GROUP_BATCHES], F32)
+            for b in range(GROUP_BATCHES):
+                batch = slice(b * TOKENS, (b + 1) * TOKENS)
+                nc.vector.scalar_tensor_tensor(
+                    out=k[:, batch],
+                    in0=live[("c", s)][:, batch],
+                    scalar=0.0,
+                    in1=live[("capped_c", s)][:, batch],
+                    op0=ALU.max,
+                    op1=ALU.add,
+                    accum_out=k_sum[:, b : b + 1],
+                )
+            q = lagged.tile([P, GROUP_TOKENS], F32)
+            nc.vector.scalar_tensor_tensor(
+                out=q[:],
+                in0=live[("a", s)][:],
+                scalar=0.0,
+                in1=live[("capped_a", s)][:],
+                op0=ALU.max,
+                op1=ALU.add,
+            )
+            k_sum_of_head = lagged.tile([P, GROUP_BATCHES, BLOCK_HEADS], F32)
+            shape = [P, GROUP_BATCHES, BLOCK_HEADS]
+            nc.vector.tensor_tensor(
+                out=k_sum_of_head[:],
+                in0=head_of_row[:].unsqueeze(1).to_broadcast(shape),
+                in1=k_sum[:].unsqueeze(2).to_broadcast(shape),
+                op=ALU.mult,
+            )
+            q_times_k = lagged.tile([P, GROUP_TOKENS], F32)
+            nc.vector.tensor_tensor(out=q_times_k[:], in0=q[:], in1=k[:], op=ALU.mult)
+            live[("q", s)] = q
+            live[("q_times_k", s)] = q_times_k
+            live[("k_sum_of_head", s)] = k_sum_of_head
+
+        def head_sums(s):
+            g, block = divmod(s, FEATURE_BLOCKS)
+            if block == 0:
+                sums = sums_psum.tile([P, 2, TILES, HEADS], F32)
+                live[("sums", g)] = sums
+            sums = live[("sums", g)]
+            heads = slice(block * BLOCK_HEADS, (block + 1) * BLOCK_HEADS)
+            for t in range(TILES):
+                tile_tokens = slice(t * P, (t + 1) * P)
+                nc.tensor.matmul(
+                    out=sums[:, 0, t, heads],
+                    lhsT=live[("q_times_k", s)][:, tile_tokens],
+                    rhs=head_of_row[:],
+                    start=True,
+                    stop=True,
+                )
+                nc.tensor.matmul(
+                    out=sums[:, 1, t, heads],
+                    lhsT=live[("q", s)][:, tile_tokens],
+                    rhs=live[("k_sum_of_head", s)][:, t // BATCH_TILES, :],
+                    start=True,
+                    stop=True,
+                )
+
+        def divide(g):
+            sums = live[("sums", g)]
+            denominator = stage.tile([P, TILES, HEADS], F32)
+            nc.vector.tensor_scalar(
+                out=denominator[:], in0=sums[:, 1], scalar1=NORM_EPS, scalar2=None, op0=ALU.add
+            )
+            inverse = stage.tile([P, TILES, HEADS], F32)
+            nc.vector.reciprocal(out=inverse[:], in_=denominator[:])
+            ratio = stage.tile([P, TILES, HEADS], F32)
+            nc.vector.tensor_tensor(out=ratio[:], in0=sums[:, 0], in1=inverse[:], op=ALU.mult)
+            live[("ratio", g)] = ratio
+
+        def value(w):
+            g, t = divmod(w, TILES)
+            b, j = divmod(t, BATCH_TILES)
+            tile_tokens = slice(w * P, (w + 1) * P)
+            v = aux_psum.tile([P, HIDDEN], F32, tag="aux")
+            nc.tensor.matmul_mx(
+                out=v[:],
+                lhsT=x_codes[:, tile_tokens].bitcast(FP8X4),
+                lhsT_scale=x_scales[:, tile_tokens],
+                rhs=wv_codes[:].bitcast(FP8X4),
+                rhs_scale=wv_scales[:],
+                start=True,
+                stop=True,
+            )
+            if j == 0:
+                z = work.tile([P, BATCH_TILES, HIDDEN], F32)
+                live[("z", g, b)] = z
+            z = live[("z", g, b)]
+            nc.vector.tensor_tensor(
+                out=z[:, j, :].rearrange("r (n d) -> r n d", n=HEADS),
+                in0=v[:].rearrange("r (n d) -> r n d", n=HEADS),
+                in1=live[("ratio", g)][:, t, :].unsqueeze(2).to_broadcast([P, HEADS, HEAD_DIM]),
+                op=ALU.mult,
+            )
+            if j == BATCH_TILES - 1:
+                nc.sync.dma_start(
+                    out=out[GROUP_BATCHES * g + b].rearrange("(r j) f -> r (j f)", j=BATCH_TILES),
+                    in_=z[:].rearrange("r j f -> r (j f)"),
+                )
+
+        regroup_weight(wk_raw, wk_grouped)
+        regroup_weight(wq_raw, wq_grouped)
+        quantise(wk_grouped, wk_codes[:], wk_scales[:])
+        quantise(wq_grouped, wq_codes[:], wq_scales[:])
+        prepare_x(0)
+        regroup_weight(wv_raw, wv_grouped)
+
+        for s in range(UNITS + VALUE_LAG):
+            if s < UNITS:
+                project(s)
+            if 0 <= s - SUMS_LAG < UNITS:
+                head_sums(s - SUMS_LAG)
+                if (s - SUMS_LAG) % FEATURE_BLOCKS == FEATURE_BLOCKS - 1:
+                    divide((s - SUMS_LAG) // FEATURE_BLOCKS)
+            if s >= VALUE_LAG:
+                value(s - VALUE_LAG)
+            if s < UNITS:
+                combine(s)
+            if s == 0:
+                quantise(wv_grouped, wv_codes[:], wv_scales[:])
+            if s % FEATURE_BLOCKS == 1 and s // FEATURE_BLOCKS + 1 < GROUPS:
+                prepare_x(s // FEATURE_BLOCKS + 1)

@@ -100,7 +100,7 @@ def tile_gatedlinearattention_pa_t_kernel(tc, hidden_states, Wq, Wk, Wv, out):
         x_codes = keep.tile([P, GROUPS * GROUP_TOKENS], U32, align_bytes=64)
         x_scales = keep.tile([P, GROUPS * GROUP_TOKENS], U8, align_bytes=64)
 
-        def prepare_x(g):
+        def transpose_x(g):
             words = x_raw[:, g, :].bitcast(F32)
             token_words = HIDDEN // 2
             x_grouped = stage.tile([P, GROUP_TOKENS * PACK], BF16, align_bytes=64)
@@ -113,14 +113,18 @@ def tile_gatedlinearattention_pa_t_kernel(tc, hidden_states, Wq, Wk, Wv, out):
                         nc.tensor.transpose(
                             xt[:, u, j * P : (j + 1) * P], words[:, first : first + P], identity[:]
                         )
-                nc.scalar.copy(
-                    out=grouped_words[:, b * 2 * TOKENS : (b + 1) * 2 * TOKENS].rearrange(
-                        "p (c u) -> p c u", u=2
-                    ),
-                    in_=xt[:].rearrange("p u c -> p c u"),
+                side_by_side = grouped_words[:, b * 2 * TOKENS : (b + 1) * 2 * TOKENS].rearrange(
+                    "p (c u) -> p c u", u=2
                 )
+                if b == 0:
+                    nc.vector.tensor_copy(out=side_by_side, in_=xt[:].rearrange("p u c -> p c u"))
+                else:
+                    nc.scalar.copy(out=side_by_side, in_=xt[:].rearrange("p u c -> p c u"))
+            live[("x_grouped", g)] = x_grouped
+
+        def quantise_x(g):
             tokens = slice(g * GROUP_TOKENS, (g + 1) * GROUP_TOKENS)
-            quantise(x_grouped, x_codes[:, tokens], x_scales[:, tokens])
+            quantise(live[("x_grouped", g)], x_codes[:, tokens], x_scales[:, tokens])
 
         live = {}
 
@@ -141,13 +145,15 @@ def tile_gatedlinearattention_pa_t_kernel(tc, hidden_states, Wq, Wk, Wv, out):
                 )
                 live[(name, s)] = acc
             for name in ("c", "a"):
-                grown = work.tile([P, GROUP_TOKENS], F32, name="exp_" + name)
-                nc.scalar.activation(out=grown[:], in_=live[(name, s)][:], func=ACT.Exp)
-                capped = work.tile([P, GROUP_TOKENS], F32, name="capped_" + name)
-                nc.gpsimd.tensor_scalar(
-                    out=capped[:], in0=grown[:], scalar1=1.0, scalar2=0.0, op0=ALU.min, op1=ALU.max
+                below = work.tile([P, GROUP_TOKENS], F32, name="below_" + name)
+                nc.scalar.activation(out=below[:], in_=live[(name, s)][:], func=ACT.Relu, scale=-1.0)
+                live[("below_" + name, s)] = below
+            for name in ("c", "a"):
+                decay = work.tile([P, GROUP_TOKENS], F32, name="decay_" + name)
+                nc.scalar.activation(
+                    out=decay[:], in_=live[("below_" + name, s)][:], func=ACT.Exp, scale=-1.0
                 )
-                live[("capped_" + name, s)] = capped
+                live[("decay_" + name, s)] = decay
 
         def combine(s):
             k = work.tile([P, GROUP_TOKENS], F32)
@@ -158,7 +164,7 @@ def tile_gatedlinearattention_pa_t_kernel(tc, hidden_states, Wq, Wk, Wv, out):
                     out=k[:, batch],
                     in0=live[("c", s)][:, batch],
                     scalar=0.0,
-                    in1=live[("capped_c", s)][:, batch],
+                    in1=live[("decay_c", s)][:, batch],
                     op0=ALU.max,
                     op1=ALU.add,
                     accum_out=k_sum[:, b : b + 1],
@@ -168,7 +174,7 @@ def tile_gatedlinearattention_pa_t_kernel(tc, hidden_states, Wq, Wk, Wv, out):
                 out=q[:],
                 in0=live[("a", s)][:],
                 scalar=0.0,
-                in1=live[("capped_a", s)][:],
+                in1=live[("decay_a", s)][:],
                 op0=ALU.max,
                 op1=ALU.add,
             )
@@ -181,7 +187,7 @@ def tile_gatedlinearattention_pa_t_kernel(tc, hidden_states, Wq, Wk, Wv, out):
                 op=ALU.mult,
             )
             q_times_k = lagged.tile([P, GROUP_TOKENS], F32)
-            nc.vector.tensor_tensor(out=q_times_k[:], in0=q[:], in1=k[:], op=ALU.mult)
+            nc.gpsimd.tensor_tensor(out=q_times_k[:], in0=q[:], in1=k[:], op=ALU.mult)
             live[("q", s)] = q
             live[("q_times_k", s)] = q_times_k
             live[("k_sum_of_head", s)] = k_sum_of_head
@@ -194,18 +200,18 @@ def tile_gatedlinearattention_pa_t_kernel(tc, hidden_states, Wq, Wk, Wv, out):
             sums = live[("sums", g)]
             heads = slice(block * BLOCK_HEADS, (block + 1) * BLOCK_HEADS)
             for t in range(TILES):
-                tile_tokens = slice(t * P, (t + 1) * P)
                 nc.tensor.matmul(
-                    out=sums[:, 0, t, heads],
-                    lhsT=live[("q_times_k", s)][:, tile_tokens],
-                    rhs=head_of_row[:],
+                    out=sums[:, 1, t, heads],
+                    lhsT=live[("q", s)][:, t * P : (t + 1) * P],
+                    rhs=live[("k_sum_of_head", s)][:, t // BATCH_TILES, :],
                     start=True,
                     stop=True,
                 )
+            for t in range(TILES):
                 nc.tensor.matmul(
-                    out=sums[:, 1, t, heads],
-                    lhsT=live[("q", s)][:, tile_tokens],
-                    rhs=live[("k_sum_of_head", s)][:, t // BATCH_TILES, :],
+                    out=sums[:, 0, t, heads],
+                    lhsT=live[("q_times_k", s)][:, t * P : (t + 1) * P],
+                    rhs=head_of_row[:],
                     start=True,
                     stop=True,
                 )
@@ -252,11 +258,12 @@ def tile_gatedlinearattention_pa_t_kernel(tc, hidden_states, Wq, Wk, Wv, out):
                     in_=z[:].rearrange("r j f -> r (j f)"),
                 )
 
+        transpose_x(0)
         regroup_weight(wk_raw, wk_grouped)
         regroup_weight(wq_raw, wq_grouped)
+        quantise_x(0)
         quantise(wk_grouped, wk_codes[:], wk_scales[:])
         quantise(wq_grouped, wq_codes[:], wq_scales[:])
-        prepare_x(0)
         regroup_weight(wv_raw, wv_grouped)
 
         for s in range(UNITS + VALUE_LAG):
@@ -272,5 +279,8 @@ def tile_gatedlinearattention_pa_t_kernel(tc, hidden_states, Wq, Wk, Wv, out):
                 combine(s)
             if s == 0:
                 quantise(wv_grouped, wv_codes[:], wv_scales[:])
-            if s % FEATURE_BLOCKS == 1 and s // FEATURE_BLOCKS + 1 < GROUPS:
-                prepare_x(s // FEATURE_BLOCKS + 1)
+            if s // FEATURE_BLOCKS + 1 < GROUPS:
+                if s % FEATURE_BLOCKS == 1:
+                    transpose_x(s // FEATURE_BLOCKS + 1)
+                if s % FEATURE_BLOCKS == 2:
+                    quantise_x(s // FEATURE_BLOCKS + 1)

@@ -22,12 +22,14 @@ GROUP_TOKENS = GROUP_BATCHES * TOKENS
 GROUPS = BATCHES // GROUP_BATCHES
 TILES = GROUP_TOKENS // P
 BATCH_TILES = TOKENS // P
-FEATURE_BLOCKS = HIDDEN // P
-BLOCK_HEADS = P // HEAD_DIM
-UNITS = GROUPS * FEATURE_BLOCKS
+SLABS = HIDDEN // P
+SLAB_DIM = HEAD_DIM // SLABS
+UNITS = GROUPS * SLABS
 
-SUMS_LAG = 2
-VALUE_LAG = FEATURE_BLOCKS - 1 + SUMS_LAG
+SUM_COLUMNS = 32
+
+SUMS_LAG = SLABS - 1 + 2
+VALUE_LAG = SUMS_LAG + TILES - 1
 
 FLOPS = 3 * 2 * BATCHES * TOKENS * HIDDEN * HIDDEN
 
@@ -38,7 +40,7 @@ def tile_gatedlinearattention_pa_t_kernel(tc, hidden_states, Wq, Wk, Wv, out):
         keep = stack.enter_context(tc.tile_pool(name="keep", bufs=1))
         stage = stack.enter_context(tc.tile_pool(name="stage", bufs=2))
         work = stack.enter_context(tc.tile_pool(name="work", bufs=3))
-        lagged = stack.enter_context(tc.tile_pool(name="lagged", bufs=SUMS_LAG + 2))
+        lagged = stack.enter_context(tc.tile_pool(name="lagged", bufs=VALUE_LAG + 1))
         proj_psum = stack.enter_context(tc.psum_pool(name="proj_psum", bufs=4))
         aux_psum = stack.enter_context(tc.psum_pool(name="aux_psum", bufs=3))
         sums_psum = stack.enter_context(tc.psum_pool(name="sums_psum", bufs=1))
@@ -65,28 +67,24 @@ def tile_gatedlinearattention_pa_t_kernel(tc, hidden_states, Wq, Wk, Wv, out):
         load_x(0)
         load_weight(Wk, wk_raw)
         load_weight(Wq, wq_raw)
+        load_x(1)
         load_weight(Wv, wv_raw)
-        for g in range(1, GROUPS):
+        for g in range(2, GROUPS):
             load_x(g)
 
         identity = keep.tile([P, P], F32)
         make_identity(nc, identity[:])
-        head_of_row = keep.tile([P, BLOCK_HEADS], F32)
+        head_of_row = keep.tile([P, SUM_COLUMNS], F32)
         nc.vector.memset(head_of_row[:], 0.0)
-        for h in range(BLOCK_HEADS):
-            nc.vector.memset(head_of_row[h * HEAD_DIM : (h + 1) * HEAD_DIM, h : h + 1], 1.0)
+        nc.vector.tensor_reduce(
+            out=head_of_row[:, 0:HEADS],
+            in_=identity[:].rearrange("f (n e) -> f n e", e=SLAB_DIM),
+            axis=mybir.AxisListType.X,
+            op=ALU.add,
+        )
         table_warmer = keep.tile([P, 1], F32)
         nc.vector.memset(table_warmer[:], 0.0)
         nc.scalar.activation(out=table_warmer[:], in_=table_warmer[:], func=ACT.Exp)
-
-        def regroup_weight(raw, grouped):
-            nc.vector.tensor_copy(
-                out=grouped[:].rearrange("p (c i t) -> p c t i", i=4, t=PACK),
-                in_=raw[:].rearrange("p (t c i) -> p c t i", t=PACK, i=4),
-            )
-
-        def quantise(grouped, codes, scales):
-            nc.vector.quantize_mx(out=codes.bitcast(FP8X4), scales=scales, in_=grouped[:])
 
         wq_grouped = keep.tile([P, HIDDEN * PACK], BF16, align_bytes=64)
         wk_grouped = keep.tile([P, HIDDEN * PACK], BF16, align_bytes=64)
@@ -99,6 +97,30 @@ def tile_gatedlinearattention_pa_t_kernel(tc, hidden_states, Wq, Wk, Wv, out):
         wv_scales = keep.tile([P, HIDDEN], U8, align_bytes=64)
         x_codes = keep.tile([P, GROUPS * GROUP_TOKENS], U32, align_bytes=64)
         x_scales = keep.tile([P, GROUPS * GROUP_TOKENS], U8, align_bytes=64)
+
+        def quantise(grouped, codes, scales):
+            nc.vector.quantize_mx(out=codes.bitcast(FP8X4), scales=scales, in_=grouped)
+
+        def quantise_slab(i):
+            columns = slice(i * P, (i + 1) * P)
+            elements = slice(i * P * PACK, (i + 1) * P * PACK)
+            for raw, grouped in ((wk_raw, wk_grouped), (wq_raw, wq_grouped)):
+                nc.vector.tensor_copy(
+                    out=grouped[:, elements].rearrange("p (n e t) -> p n e t", n=HEADS, t=PACK),
+                    in_=raw[:].rearrange(
+                        "p (t n i e) -> p i n e t", t=PACK, n=HEADS, i=SLABS
+                    )[:, i],
+                )
+            quantise(wk_grouped[:, elements], wk_codes[:, columns], wk_scales[:, columns])
+            quantise(wq_grouped[:, elements], wq_codes[:, columns], wq_scales[:, columns])
+
+        def regroup_wv():
+            nc.vector.tensor_copy(
+                out=wv_grouped[:].rearrange("p (c i t) -> p c t i", i=4, t=PACK),
+                in_=wv_raw[:].rearrange("p (t c i) -> p c t i", t=PACK, i=4),
+            )
+
+        live = {}
 
         def transpose_x(g):
             words = x_raw[:, g, :].bitcast(F32)
@@ -124,20 +146,18 @@ def tile_gatedlinearattention_pa_t_kernel(tc, hidden_states, Wq, Wk, Wv, out):
 
         def quantise_x(g):
             tokens = slice(g * GROUP_TOKENS, (g + 1) * GROUP_TOKENS)
-            quantise(live[("x_grouped", g)], x_codes[:, tokens], x_scales[:, tokens])
-
-        live = {}
+            quantise(live[("x_grouped", g)][:], x_codes[:, tokens], x_scales[:, tokens])
 
         def project(s):
-            g, block = divmod(s, FEATURE_BLOCKS)
+            g, i = divmod(s, SLABS)
             tokens = slice(g * GROUP_TOKENS, (g + 1) * GROUP_TOKENS)
-            features = slice(block * P, (block + 1) * P)
+            columns = slice(i * P, (i + 1) * P)
             for name, codes, scales in (("c", wk_codes, wk_scales), ("a", wq_codes, wq_scales)):
                 acc = proj_psum.tile([P, GROUP_TOKENS], F32, tag="proj", name="acc_" + name)
                 nc.tensor.matmul_mx(
                     out=acc[:],
-                    lhsT=codes[:, features].bitcast(FP8X4),
-                    lhsT_scale=scales[:, features],
+                    lhsT=codes[:, columns].bitcast(FP8X4),
+                    lhsT_scale=scales[:, columns],
                     rhs=x_codes[:, tokens].bitcast(FP8X4),
                     rhs_scale=x_scales[:, tokens],
                     start=True,
@@ -156,8 +176,9 @@ def tile_gatedlinearattention_pa_t_kernel(tc, hidden_states, Wq, Wk, Wv, out):
                 live[("decay_" + name, s)] = decay
 
         def combine(s):
+            g, i = divmod(s, SLABS)
             k = work.tile([P, GROUP_TOKENS], F32)
-            k_sum = lagged.tile([P, GROUP_BATCHES], F32)
+            k_sum = stage.tile([P, GROUP_BATCHES], F32)
             for b in range(GROUP_BATCHES):
                 batch = slice(b * TOKENS, (b + 1) * TOKENS)
                 nc.vector.scalar_tensor_tensor(
@@ -178,54 +199,63 @@ def tile_gatedlinearattention_pa_t_kernel(tc, hidden_states, Wq, Wk, Wv, out):
                 op0=ALU.max,
                 op1=ALU.add,
             )
-            k_sum_of_head = lagged.tile([P, GROUP_BATCHES, BLOCK_HEADS], F32)
-            shape = [P, GROUP_BATCHES, BLOCK_HEADS]
+            k_sum_of_head = lagged.tile([P, GROUP_BATCHES, SUM_COLUMNS], F32)
+            shape = [P, GROUP_BATCHES, SUM_COLUMNS]
             nc.vector.tensor_tensor(
                 out=k_sum_of_head[:],
                 in0=head_of_row[:].unsqueeze(1).to_broadcast(shape),
                 in1=k_sum[:].unsqueeze(2).to_broadcast(shape),
                 op=ALU.mult,
             )
-            q_times_k = lagged.tile([P, GROUP_TOKENS], F32)
-            nc.gpsimd.tensor_tensor(out=q_times_k[:], in0=q[:], in1=k[:], op=ALU.mult)
             live[("q", s)] = q
-            live[("q_times_k", s)] = q_times_k
             live[("k_sum_of_head", s)] = k_sum_of_head
+            if i == 0:
+                q_times_k = work.tile([P, GROUP_TOKENS], F32)
+                nc.gpsimd.tensor_tensor(out=q_times_k[:], in0=q[:], in1=k[:], op=ALU.mult)
+                live[("q_times_k", g)] = q_times_k
+            else:
+                q_times_k = live[("q_times_k", g)]
+                slab_product = work.tile([P, GROUP_TOKENS], F32)
+                nc.gpsimd.tensor_tensor(out=slab_product[:], in0=q[:], in1=k[:], op=ALU.mult)
+                nc.gpsimd.tensor_tensor(
+                    out=q_times_k[:], in0=q_times_k[:], in1=slab_product[:], op=ALU.add
+                )
 
-        def head_sums(s):
-            g, block = divmod(s, FEATURE_BLOCKS)
-            if block == 0:
-                sums = sums_psum.tile([P, 2, TILES, HEADS], F32)
+        def head_sums(h):
+            g, t = divmod(h, TILES)
+            if t == 0:
+                sums = sums_psum.tile([P, 2, TILES, SUM_COLUMNS], F32)
                 live[("sums", g)] = sums
             sums = live[("sums", g)]
-            heads = slice(block * BLOCK_HEADS, (block + 1) * BLOCK_HEADS)
-            for t in range(TILES):
+            tile_tokens = slice(t * P, (t + 1) * P)
+            for i in range(SLABS):
                 nc.tensor.matmul(
-                    out=sums[:, 1, t, heads],
-                    lhsT=live[("q", s)][:, t * P : (t + 1) * P],
-                    rhs=live[("k_sum_of_head", s)][:, t // BATCH_TILES, :],
-                    start=True,
-                    stop=True,
+                    out=sums[:, 1, t, :],
+                    lhsT=live[("q", g * SLABS + i)][:, tile_tokens],
+                    rhs=live[("k_sum_of_head", g * SLABS + i)][:, t // BATCH_TILES, :],
+                    start=(i == 0),
+                    stop=(i == SLABS - 1),
                 )
-            for t in range(TILES):
-                nc.tensor.matmul(
-                    out=sums[:, 0, t, heads],
-                    lhsT=live[("q_times_k", s)][:, t * P : (t + 1) * P],
-                    rhs=head_of_row[:],
-                    start=True,
-                    stop=True,
-                )
+            nc.tensor.matmul(
+                out=sums[:, 0, t, :],
+                lhsT=live[("q_times_k", g)][:, tile_tokens],
+                rhs=head_of_row[:],
+                start=True,
+                stop=True,
+            )
 
         def divide(g):
             sums = live[("sums", g)]
             denominator = stage.tile([P, TILES, HEADS], F32)
             nc.vector.tensor_scalar(
-                out=denominator[:], in0=sums[:, 1], scalar1=NORM_EPS, scalar2=None, op0=ALU.add
+                out=denominator[:], in0=sums[:, 1, :, 0:HEADS], scalar1=NORM_EPS, scalar2=None, op0=ALU.add
             )
             inverse = stage.tile([P, TILES, HEADS], F32)
             nc.vector.reciprocal(out=inverse[:], in_=denominator[:])
             ratio = stage.tile([P, TILES, HEADS], F32)
-            nc.vector.tensor_tensor(out=ratio[:], in0=sums[:, 0], in1=inverse[:], op=ALU.mult)
+            nc.vector.tensor_tensor(
+                out=ratio[:], in0=sums[:, 0, :, 0:HEADS], in1=inverse[:], op=ALU.mult
+            )
             live[("ratio", g)] = ratio
 
         def value(w):
@@ -259,28 +289,28 @@ def tile_gatedlinearattention_pa_t_kernel(tc, hidden_states, Wq, Wk, Wv, out):
                 )
 
         transpose_x(0)
-        regroup_weight(wk_raw, wk_grouped)
-        regroup_weight(wq_raw, wq_grouped)
+        quantise_slab(0)
         quantise_x(0)
-        quantise(wk_grouped, wk_codes[:], wk_scales[:])
-        quantise(wq_grouped, wq_codes[:], wq_scales[:])
-        regroup_weight(wv_raw, wv_grouped)
 
         for s in range(UNITS + VALUE_LAG):
             if s < UNITS:
                 project(s)
+            if s + 1 < SLABS:
+                quantise_slab(s + 1)
             if 0 <= s - SUMS_LAG < UNITS:
                 head_sums(s - SUMS_LAG)
-                if (s - SUMS_LAG) % FEATURE_BLOCKS == FEATURE_BLOCKS - 1:
-                    divide((s - SUMS_LAG) // FEATURE_BLOCKS)
+                if (s - SUMS_LAG) % TILES == TILES - 1:
+                    divide((s - SUMS_LAG) // TILES)
             if s >= VALUE_LAG:
                 value(s - VALUE_LAG)
             if s < UNITS:
                 combine(s)
-            if s == 0:
-                quantise(wv_grouped, wv_codes[:], wv_scales[:])
-            if s // FEATURE_BLOCKS + 1 < GROUPS:
-                if s % FEATURE_BLOCKS == 1:
-                    transpose_x(s // FEATURE_BLOCKS + 1)
-                if s % FEATURE_BLOCKS == 2:
-                    quantise_x(s // FEATURE_BLOCKS + 1)
+            if s == SLABS - 1:
+                regroup_wv()
+            if s == SLABS:
+                quantise(wv_grouped[:], wv_codes[:], wv_scales[:])
+            if s // SLABS + 1 < GROUPS:
+                if s % SLABS == 1:
+                    transpose_x(s // SLABS + 1)
+                if s % SLABS == 2:
+                    quantise_x(s // SLABS + 1)

@@ -26,7 +26,7 @@ SLABS = HIDDEN // P
 SLAB_DIM = HEAD_DIM // SLABS
 UNITS = GROUPS * SLABS
 
-SUM_COLUMNS = 32
+SUM_COLUMNS = 64
 
 SUMS_LAG = SLABS - 1 + 2
 VALUE_LAG = SUMS_LAG + TILES - 1

@@ -28,8 +28,8 @@ UNITS = GROUPS * SLABS
 
 SUM_COLUMNS = 64
 
-SUMS_LAG = SLABS - 1 + 2
-VALUE_LAG = SUMS_LAG + TILES - 1
+SUMS_LAG = SLABS - 1 + 3
+VALUE_LAG = SUMS_LAG + TILES
 
 FLOPS = 3 * 2 * BATCHES * TOKENS * HIDDEN * HIDDEN
 
@@ -209,17 +209,17 @@ def tile_gatedlinearattention_pa_t_kernel(tc, hidden_states, Wq, Wk, Wv, out):
             )
             live[("q", s)] = q
             live[("k_sum_of_head", s)] = k_sum_of_head
-            if i == 0:
-                q_times_k = work.tile([P, GROUP_TOKENS], F32)
-                nc.gpsimd.tensor_tensor(out=q_times_k[:], in0=q[:], in1=k[:], op=ALU.mult)
-                live[("q_times_k", g)] = q_times_k
-            else:
-                q_times_k = live[("q_times_k", g)]
-                slab_product = work.tile([P, GROUP_TOKENS], F32)
-                nc.gpsimd.tensor_tensor(out=slab_product[:], in0=q[:], in1=k[:], op=ALU.mult)
+            if i >= 2:
+                summed_products = live[("product", s - i)]
                 nc.gpsimd.tensor_tensor(
-                    out=q_times_k[:], in0=q_times_k[:], in1=slab_product[:], op=ALU.add
+                    out=summed_products[:],
+                    in0=summed_products[:],
+                    in1=live[("product", s - 1)][:],
+                    op=ALU.add,
                 )
+            product = lagged.tile([P, GROUP_TOKENS], F32)
+            nc.gpsimd.tensor_tensor(out=product[:], in0=q[:], in1=k[:], op=ALU.mult)
+            live[("product", s)] = product
 
         def head_sums(h):
             g, t = divmod(h, TILES)
@@ -238,9 +238,16 @@ def tile_gatedlinearattention_pa_t_kernel(tc, hidden_states, Wq, Wk, Wv, out):
                 )
             nc.tensor.matmul(
                 out=sums[:, 0, t, :],
-                lhsT=live[("q_times_k", g)][:, tile_tokens],
+                lhsT=live[("product", g * SLABS)][:, tile_tokens],
                 rhs=head_of_row[:],
                 start=True,
+                stop=False,
+            )
+            nc.tensor.matmul(
+                out=sums[:, 0, t, :],
+                lhsT=live[("product", g * SLABS + SLABS - 1)][:, tile_tokens],
+                rhs=head_of_row[:],
+                start=False,
                 stop=True,
             )
 
@@ -297,12 +304,12 @@ def tile_gatedlinearattention_pa_t_kernel(tc, hidden_states, Wq, Wk, Wv, out):
                 project(s)
             if s + 1 < SLABS:
                 quantise_slab(s + 1)
+            if s >= VALUE_LAG:
+                value(s - VALUE_LAG)
             if 0 <= s - SUMS_LAG < UNITS:
                 head_sums(s - SUMS_LAG)
                 if (s - SUMS_LAG) % TILES == TILES - 1:
                     divide((s - SUMS_LAG) // TILES)
-            if s >= VALUE_LAG:
-                value(s - VALUE_LAG)
             if s < UNITS:
                 combine(s)
             if s == SLABS - 1:
@@ -310,7 +317,7 @@ def tile_gatedlinearattention_pa_t_kernel(tc, hidden_states, Wq, Wk, Wv, out):
             if s == SLABS:
                 quantise(wv_grouped[:], wv_codes[:], wv_scales[:])
             if s // SLABS + 1 < GROUPS:
-                if s % SLABS == 1:
+                if s % SLABS == 0:
                     transpose_x(s // SLABS + 1)
-                if s % SLABS == 2:
+                if s % SLABS == 1:
                     quantise_x(s // SLABS + 1)

@@ -42,8 +42,8 @@ def tile_gatedlinearattention_pa_t_kernel(tc, hidden_states, Wq, Wk, Wv, out):
         work = stack.enter_context(tc.tile_pool(name="work", bufs=3))
         lagged = stack.enter_context(tc.tile_pool(name="lagged", bufs=VALUE_LAG + 1))
         proj_psum = stack.enter_context(tc.psum_pool(name="proj_psum", bufs=4))
-        aux_psum = stack.enter_context(tc.psum_pool(name="aux_psum", bufs=3))
-        sums_psum = stack.enter_context(tc.psum_pool(name="sums_psum", bufs=1))
+        aux_psum = stack.enter_context(tc.psum_pool(name="aux_psum", bufs=2))
+        sums_psum = stack.enter_context(tc.psum_pool(name="sums_psum", bufs=2))
         stack.enter_context(tc.manual_schedule())
 
         x_raw = keep.tile([P, GROUPS, GROUP_TOKENS * HIDDEN // P], BF16)
@@ -209,17 +209,23 @@ def tile_gatedlinearattention_pa_t_kernel(tc, hidden_states, Wq, Wk, Wv, out):
             )
             live[("q", s)] = q
             live[("k_sum_of_head", s)] = k_sum_of_head
-            if i >= 2:
-                summed_products = live[("product", s - i)]
-                nc.gpsimd.tensor_tensor(
+            product = lagged.tile([P, GROUP_TOKENS], F32)
+            product_engine(s).tensor_tensor(out=product[:], in0=q[:], in1=k[:], op=ALU.mult)
+            live[("product", s)] = product
+
+        def product_engine(s):
+            return nc.vector if s == UNITS - 1 else nc.gpsimd
+
+        def add_product(s):
+            g, i = divmod(s, SLABS)
+            if i > 0:
+                summed_products = live[("product", g * SLABS)]
+                product_engine(s).tensor_tensor(
                     out=summed_products[:],
                     in0=summed_products[:],
-                    in1=live[("product", s - 1)][:],
+                    in1=live[("product", s)][:],
                     op=ALU.add,
                 )
-            product = lagged.tile([P, GROUP_TOKENS], F32)
-            nc.gpsimd.tensor_tensor(out=product[:], in0=q[:], in1=k[:], op=ALU.mult)
-            live[("product", s)] = product
 
         def head_sums(h):
             g, t = divmod(h, TILES)
@@ -241,13 +247,6 @@ def tile_gatedlinearattention_pa_t_kernel(tc, hidden_states, Wq, Wk, Wv, out):
                 lhsT=live[("product", g * SLABS)][:, tile_tokens],
                 rhs=head_of_row[:],
                 start=True,
-                stop=False,
-            )
-            nc.tensor.matmul(
-                out=sums[:, 0, t, :],
-                lhsT=live[("product", g * SLABS + SLABS - 1)][:, tile_tokens],
-                rhs=head_of_row[:],
-                start=False,
                 stop=True,
             )
 
@@ -269,7 +268,10 @@ def tile_gatedlinearattention_pa_t_kernel(tc, hidden_states, Wq, Wk, Wv, out):
             g, t = divmod(w, TILES)
             b, j = divmod(t, BATCH_TILES)
             tile_tokens = slice(w * P, (w + 1) * P)
-            v = aux_psum.tile([P, HIDDEN], F32, tag="aux")
+            if g < GROUPS - 1:
+                v = aux_psum.tile([P, HIDDEN], F32, tag="aux")
+            else:
+                v = proj_psum.tile([P, HIDDEN], F32, tag="proj")
             nc.tensor.matmul_mx(
                 out=v[:],
                 lhsT=x_codes[:, tile_tokens].bitcast(FP8X4),
@@ -310,6 +312,8 @@ def tile_gatedlinearattention_pa_t_kernel(tc, hidden_states, Wq, Wk, Wv, out):
                 head_sums(s - SUMS_LAG)
                 if (s - SUMS_LAG) % TILES == TILES - 1:
                     divide((s - SUMS_LAG) // TILES)
+            if 1 <= s <= UNITS:
+                add_product(s - 1)
             if s < UNITS:
                 combine(s)
             if s == SLABS - 1:

@@ -42,8 +42,8 @@ def tile_gatedlinearattention_pa_t_kernel(tc, hidden_states, Wq, Wk, Wv, out):
         work = stack.enter_context(tc.tile_pool(name="work", bufs=3))
         lagged = stack.enter_context(tc.tile_pool(name="lagged", bufs=VALUE_LAG + 1))
         proj_psum = stack.enter_context(tc.psum_pool(name="proj_psum", bufs=4))
-        aux_psum = stack.enter_context(tc.psum_pool(name="aux_psum", bufs=2))
-        sums_psum = stack.enter_context(tc.psum_pool(name="sums_psum", bufs=2))
+        aux_psum = stack.enter_context(tc.psum_pool(name="aux_psum", bufs=3))
+        sums_psum = stack.enter_context(tc.psum_pool(name="sums_psum", bufs=1))
         stack.enter_context(tc.manual_schedule())
 
         x_raw = keep.tile([P, GROUPS, GROUP_TOKENS * HIDDEN // P], BF16)
@@ -210,22 +210,9 @@ def tile_gatedlinearattention_pa_t_kernel(tc, hidden_states, Wq, Wk, Wv, out):
             live[("q", s)] = q
             live[("k_sum_of_head", s)] = k_sum_of_head
             product = lagged.tile([P, GROUP_TOKENS], F32)
-            product_engine(s).tensor_tensor(out=product[:], in0=q[:], in1=k[:], op=ALU.mult)
+            product_engine = nc.vector if s == UNITS - 1 else nc.gpsimd
+            product_engine.tensor_tensor(out=product[:], in0=q[:], in1=k[:], op=ALU.mult)
             live[("product", s)] = product
-
-        def product_engine(s):
-            return nc.vector if s == UNITS - 1 else nc.gpsimd
-
-        def add_product(s):
-            g, i = divmod(s, SLABS)
-            if i > 0:
-                summed_products = live[("product", g * SLABS)]
-                product_engine(s).tensor_tensor(
-                    out=summed_products[:],
-                    in0=summed_products[:],
-                    in1=live[("product", s)][:],
-                    op=ALU.add,
-                )
 
         def head_sums(h):
             g, t = divmod(h, TILES)
@@ -242,13 +229,14 @@ def tile_gatedlinearattention_pa_t_kernel(tc, hidden_states, Wq, Wk, Wv, out):
                     start=(i == 0),
                     stop=(i == SLABS - 1),
                 )
-            nc.tensor.matmul(
-                out=sums[:, 0, t, :],
-                lhsT=live[("product", g * SLABS)][:, tile_tokens],
-                rhs=head_of_row[:],
-                start=True,
-                stop=True,
-            )
+            for i in range(SLABS):
+                nc.tensor.matmul(
+                    out=sums[:, 0, t, :],
+                    lhsT=live[("product", g * SLABS + i)][:, tile_tokens],
+                    rhs=head_of_row[:],
+                    start=(i == 0),
+                    stop=(i == SLABS - 1),
+                )
 
         def divide(g):
             sums = live[("sums", g)]
@@ -268,10 +256,7 @@ def tile_gatedlinearattention_pa_t_kernel(tc, hidden_states, Wq, Wk, Wv, out):
             g, t = divmod(w, TILES)
             b, j = divmod(t, BATCH_TILES)
             tile_tokens = slice(w * P, (w + 1) * P)
-            if g < GROUPS - 1:
-                v = aux_psum.tile([P, HIDDEN], F32, tag="aux")
-            else:
-                v = proj_psum.tile([P, HIDDEN], F32, tag="proj")
+            v = aux_psum.tile([P, HIDDEN], F32, tag="aux")
             nc.tensor.matmul_mx(
                 out=v[:],
                 lhsT=x_codes[:, tile_tokens].bitcast(FP8X4),
@@ -312,8 +297,6 @@ def tile_gatedlinearattention_pa_t_kernel(tc, hidden_states, Wq, Wk, Wv, out):
                 head_sums(s - SUMS_LAG)
                 if (s - SUMS_LAG) % TILES == TILES - 1:
                     divide((s - SUMS_LAG) // TILES)
-            if 1 <= s <= UNITS:
-                add_product(s - 1)
             if s < UNITS:
                 combine(s)
             if s == SLABS - 1:

@@ -30,6 +30,7 @@ SUM_COLUMNS = 64
 
 SUMS_LAG = SLABS - 1 + 3
 VALUE_LAG = SUMS_LAG + TILES
+ADD_LAG = 2
 
 FLOPS = 3 * 2 * BATCHES * TOKENS * HIDDEN * HIDDEN
 
@@ -42,8 +43,8 @@ def tile_gatedlinearattention_pa_t_kernel(tc, hidden_states, Wq, Wk, Wv, out):
         work = stack.enter_context(tc.tile_pool(name="work", bufs=3))
         lagged = stack.enter_context(tc.tile_pool(name="lagged", bufs=VALUE_LAG + 1))
         proj_psum = stack.enter_context(tc.psum_pool(name="proj_psum", bufs=4))
-        aux_psum = stack.enter_context(tc.psum_pool(name="aux_psum", bufs=3))
-        sums_psum = stack.enter_context(tc.psum_pool(name="sums_psum", bufs=1))
+        aux_psum = stack.enter_context(tc.psum_pool(name="aux_psum", bufs=2))
+        sums_psum = stack.enter_context(tc.psum_pool(name="sums_psum", bufs=2))
         stack.enter_context(tc.manual_schedule())
 
         x_raw = keep.tile([P, GROUPS, GROUP_TOKENS * HIDDEN // P], BF16)
@@ -214,6 +215,14 @@ def tile_gatedlinearattention_pa_t_kernel(tc, hidden_states, Wq, Wk, Wv, out):
             product_engine.tensor_tensor(out=product[:], in0=q[:], in1=k[:], op=ALU.mult)
             live[("product", s)] = product
 
+        def add_products(engine, into, unit):
+            engine.tensor_tensor(
+                out=live[("product", into)][:],
+                in0=live[("product", into)][:],
+                in1=live[("product", unit)][:],
+                op=ALU.add,
+            )
+
         def head_sums(h):
             g, t = divmod(h, TILES)
             if t == 0:
@@ -229,14 +238,13 @@ def tile_gatedlinearattention_pa_t_kernel(tc, hidden_states, Wq, Wk, Wv, out):
                     start=(i == 0),
                     stop=(i == SLABS - 1),
                 )
-            for i in range(SLABS):
-                nc.tensor.matmul(
-                    out=sums[:, 0, t, :],
-                    lhsT=live[("product", g * SLABS + i)][:, tile_tokens],
-                    rhs=head_of_row[:],
-                    start=(i == 0),
-                    stop=(i == SLABS - 1),
-                )
+            nc.tensor.matmul(
+                out=sums[:, 0, t, :],
+                lhsT=live[("product", g * SLABS)][:, tile_tokens],
+                rhs=head_of_row[:],
+                start=True,
+                stop=True,
+            )
 
         def divide(g):
             sums = live[("sums", g)]
@@ -256,7 +264,10 @@ def tile_gatedlinearattention_pa_t_kernel(tc, hidden_states, Wq, Wk, Wv, out):
             g, t = divmod(w, TILES)
             b, j = divmod(t, BATCH_TILES)
             tile_tokens = slice(w * P, (w + 1) * P)
-            v = aux_psum.tile([P, HIDDEN], F32, tag="aux")
+            if g < GROUPS - 1:
+                v = aux_psum.tile([P, HIDDEN], F32, tag="aux")
+            else:
+                v = proj_psum.tile([P, HIDDEN], F32, tag="proj")
             nc.tensor.matmul_mx(
                 out=v[:],
                 lhsT=x_codes[:, tile_tokens].bitcast(FP8X4),
@@ -297,8 +308,16 @@ def tile_gatedlinearattention_pa_t_kernel(tc, hidden_states, Wq, Wk, Wv, out):
                 head_sums(s - SUMS_LAG)
                 if (s - SUMS_LAG) % TILES == TILES - 1:
                     divide((s - SUMS_LAG) // TILES)
+            if s < UNITS and s % SLABS == 2:
+                add_products(nc.gpsimd, s - 2, s - 1)
+            last_unit = s - ADD_LAG
+            group_is_multiplied = 0 <= last_unit < UNITS and last_unit % SLABS == SLABS - 1
+            if group_is_multiplied:
+                add_products(nc.vector, last_unit - 1, last_unit)
             if s < UNITS:
                 combine(s)
+            if group_is_multiplied:
+                add_products(nc.vector, last_unit - 3, last_unit - 1)
             if s == SLABS - 1:
                 regroup_wv()
             if s == SLABS:

from contextlib import ExitStack

import concourse.mybir as mybir
from concourse.masks import make_identity

F32 = mybir.dt.float32
BF16 = mybir.dt.bfloat16
U32 = mybir.dt.uint32
U8 = mybir.dt.uint8
FP8X4 = mybir.dt.float8_e4m3fn_x4
ALU = mybir.AluOpType
ACT = mybir.ActivationFunctionType

P = 128
PACK = 4
BATCHES, TOKENS, HIDDEN, HEADS = 16, 256, 512, 8
HEAD_DIM = HIDDEN // HEADS
NORM_EPS = 1e-6

GROUP_BATCHES = 2
GROUP_TOKENS = GROUP_BATCHES * TOKENS
GROUPS = BATCHES // GROUP_BATCHES
TILES = GROUP_TOKENS // P
BATCH_TILES = TOKENS // P
SLABS = HIDDEN // P
SLAB_DIM = HEAD_DIM // SLABS
UNITS = GROUPS * SLABS

SUM_COLUMNS = 64

SUMS_LAG = SLABS - 1 + 3
VALUE_LAG = SUMS_LAG + TILES
ADD_LAG = 2

FLOPS = 3 * 2 * BATCHES * TOKENS * HIDDEN * HIDDEN


def tile_gatedlinearattention_pa_t_kernel(tc, hidden_states, Wq, Wk, Wv, out):
    nc = tc.nc
    with ExitStack() as stack:
        keep = stack.enter_context(tc.tile_pool(name="keep", bufs=1))
        stage = stack.enter_context(tc.tile_pool(name="stage", bufs=2))
        work = stack.enter_context(tc.tile_pool(name="work", bufs=3))
        lagged = stack.enter_context(tc.tile_pool(name="lagged", bufs=VALUE_LAG + 1))
        proj_psum = stack.enter_context(tc.psum_pool(name="proj_psum", bufs=4))
        aux_psum = stack.enter_context(tc.psum_pool(name="aux_psum", bufs=2))
        sums_psum = stack.enter_context(tc.psum_pool(name="sums_psum", bufs=2))
        stack.enter_context(tc.manual_schedule())

        x_raw = keep.tile([P, GROUPS, GROUP_TOKENS * HIDDEN // P], BF16)

        def load_x(g):
            batches = hidden_states[GROUP_BATCHES * g : GROUP_BATCHES * (g + 1)]
            nc.sync.dma_start(
                out=x_raw[:, g, :].rearrange("r (b w) -> r b w", b=GROUP_BATCHES),
                in_=batches.rearrange("b (r j) k -> r b (j k)", j=BATCH_TILES),
            )

        def load_weight(w, raw):
            nc.sync.dma_start(
                out=raw[:].rearrange("p (u w) -> p u w", u=2),
                in_=w.rearrange("(u p e) n -> p u (e n)", u=2, e=2),
            )

        wq_raw = keep.tile([P, PACK * HIDDEN], BF16)
        wk_raw = keep.tile([P, PACK * HIDDEN], BF16)
        wv_raw = keep.tile([P, PACK * HIDDEN], BF16)
        load_x(0)
        load_weight(Wk, wk_raw)
        load_weight(Wq, wq_raw)
        load_x(1)
        load_weight(Wv, wv_raw)
        for g in range(2, GROUPS):
            load_x(g)

        identity = keep.tile([P, P], F32)
        make_identity(nc, identity[:])
        head_of_row = keep.tile([P, SUM_COLUMNS], F32)
        nc.vector.memset(head_of_row[:], 0.0)
        nc.vector.tensor_reduce(
            out=head_of_row[:, 0:HEADS],
            in_=identity[:].rearrange("f (n e) -> f n e", e=SLAB_DIM),
            axis=mybir.AxisListType.X,
            op=ALU.add,
        )
        table_warmer = keep.tile([P, 1], F32)
        nc.vector.memset(table_warmer[:], 0.0)
        nc.scalar.activation(out=table_warmer[:], in_=table_warmer[:], func=ACT.Exp)

        wq_grouped = keep.tile([P, HIDDEN * PACK], BF16, align_bytes=64)
        wk_grouped = keep.tile([P, HIDDEN * PACK], BF16, align_bytes=64)
        wv_grouped = keep.tile([P, HIDDEN * PACK], BF16, align_bytes=64)
        wq_codes = keep.tile([P, HIDDEN], U32, align_bytes=64)
        wk_codes = keep.tile([P, HIDDEN], U32, align_bytes=64)
        wv_codes = keep.tile([P, HIDDEN], U32, align_bytes=64)
        wq_scales = keep.tile([P, HIDDEN], U8, align_bytes=64)
        wk_scales = keep.tile([P, HIDDEN], U8, align_bytes=64)
        wv_scales = keep.tile([P, HIDDEN], U8, align_bytes=64)
        x_codes = keep.tile([P, GROUPS * GROUP_TOKENS], U32, align_bytes=64)
        x_scales = keep.tile([P, GROUPS * GROUP_TOKENS], U8, align_bytes=64)

        def quantise(grouped, codes, scales):
            nc.vector.quantize_mx(out=codes.bitcast(FP8X4), scales=scales, in_=grouped)

        def quantise_slab(i):
            columns = slice(i * P, (i + 1) * P)
            elements = slice(i * P * PACK, (i + 1) * P * PACK)
            for raw, grouped in ((wk_raw, wk_grouped), (wq_raw, wq_grouped)):
                nc.vector.tensor_copy(
                    out=grouped[:, elements].rearrange("p (n e t) -> p n e t", n=HEADS, t=PACK),
                    in_=raw[:].rearrange(
                        "p (t n i e) -> p i n e t", t=PACK, n=HEADS, i=SLABS
                    )[:, i],
                )
            quantise(wk_grouped[:, elements], wk_codes[:, columns], wk_scales[:, columns])
            quantise(wq_grouped[:, elements], wq_codes[:, columns], wq_scales[:, columns])

        def regroup_wv():
            nc.vector.tensor_copy(
                out=wv_grouped[:].rearrange("p (c i t) -> p c t i", i=4, t=PACK),
                in_=wv_raw[:].rearrange("p (t c i) -> p c t i", t=PACK, i=4),
            )

        live = {}

        def transpose_x(g):
            words = x_raw[:, g, :].bitcast(F32)
            token_words = HIDDEN // 2
            x_grouped = stage.tile([P, GROUP_TOKENS * PACK], BF16, align_bytes=64)
            grouped_words = x_grouped[:].bitcast(F32)
            for b in range(GROUP_BATCHES):
                xt = aux_psum.tile([P, 2, TOKENS], F32, tag="aux")
                for j in range(BATCH_TILES):
                    for u in range(2):
                        first = (b * BATCH_TILES + j) * token_words + u * P
                        nc.tensor.transpose(
                            xt[:, u, j * P : (j + 1) * P], words[:, first : first + P], identity[:]
                        )
                side_by_side = grouped_words[:, b * 2 * TOKENS : (b + 1) * 2 * TOKENS].rearrange(
                    "p (c u) -> p c u", u=2
                )
                if b == 0:
                    nc.vector.tensor_copy(out=side_by_side, in_=xt[:].rearrange("p u c -> p c u"))
                else:
                    nc.scalar.copy(out=side_by_side, in_=xt[:].rearrange("p u c -> p c u"))
            live[("x_grouped", g)] = x_grouped

        def quantise_x(g):
            tokens = slice(g * GROUP_TOKENS, (g + 1) * GROUP_TOKENS)
            quantise(live[("x_grouped", g)][:], x_codes[:, tokens], x_scales[:, tokens])

        def project(s):
            g, i = divmod(s, SLABS)
            tokens = slice(g * GROUP_TOKENS, (g + 1) * GROUP_TOKENS)
            columns = slice(i * P, (i + 1) * P)
            for name, codes, scales in (("c", wk_codes, wk_scales), ("a", wq_codes, wq_scales)):
                acc = proj_psum.tile([P, GROUP_TOKENS], F32, tag="proj", name="acc_" + name)
                nc.tensor.matmul_mx(
                    out=acc[:],
                    lhsT=codes[:, columns].bitcast(FP8X4),
                    lhsT_scale=scales[:, columns],
                    rhs=x_codes[:, tokens].bitcast(FP8X4),
                    rhs_scale=x_scales[:, tokens],
                    start=True,
                    stop=True,
                )
                live[(name, s)] = acc
            for name in ("c", "a"):
                below = work.tile([P, GROUP_TOKENS], F32, name="below_" + name)
                nc.scalar.activation(out=below[:], in_=live[(name, s)][:], func=ACT.Relu, scale=-1.0)
                live[("below_" + name, s)] = below
            for name in ("c", "a"):
                decay = work.tile([P, GROUP_TOKENS], F32, name="decay_" + name)
                nc.scalar.activation(
                    out=decay[:], in_=live[("below_" + name, s)][:], func=ACT.Exp, scale=-1.0
                )
                live[("decay_" + name, s)] = decay

        def combine(s):
            g, i = divmod(s, SLABS)
            k = work.tile([P, GROUP_TOKENS], F32)
            k_sum = stage.tile([P, GROUP_BATCHES], F32)
            for b in range(GROUP_BATCHES):
                batch = slice(b * TOKENS, (b + 1) * TOKENS)
                nc.vector.scalar_tensor_tensor(
                    out=k[:, batch],
                    in0=live[("c", s)][:, batch],
                    scalar=0.0,
                    in1=live[("decay_c", s)][:, batch],
                    op0=ALU.max,
                    op1=ALU.add,
                    accum_out=k_sum[:, b : b + 1],
                )
            q = lagged.tile([P, GROUP_TOKENS], F32)
            nc.vector.scalar_tensor_tensor(
                out=q[:],
                in0=live[("a", s)][:],
                scalar=0.0,
                in1=live[("decay_a", s)][:],
                op0=ALU.max,
                op1=ALU.add,
            )
            k_sum_of_head = lagged.tile([P, GROUP_BATCHES, SUM_COLUMNS], F32)
            shape = [P, GROUP_BATCHES, SUM_COLUMNS]
            nc.vector.tensor_tensor(
                out=k_sum_of_head[:],
                in0=head_of_row[:].unsqueeze(1).to_broadcast(shape),
                in1=k_sum[:].unsqueeze(2).to_broadcast(shape),
                op=ALU.mult,
            )
            live[("q", s)] = q
            live[("k_sum_of_head", s)] = k_sum_of_head
            product = lagged.tile([P, GROUP_TOKENS], F32)
            product_engine = nc.vector if s == UNITS - 1 else nc.gpsimd
            product_engine.tensor_tensor(out=product[:], in0=q[:], in1=k[:], op=ALU.mult)
            live[("product", s)] = product

        def add_products(engine, into, unit):
            engine.tensor_tensor(
                out=live[("product", into)][:],
                in0=live[("product", into)][:],
                in1=live[("product", unit)][:],
                op=ALU.add,
            )

        def head_sums(h):
            g, t = divmod(h, TILES)
            if t == 0:
                sums = sums_psum.tile([P, 2, TILES, SUM_COLUMNS], F32)
                live[("sums", g)] = sums
            sums = live[("sums", g)]
            tile_tokens = slice(t * P, (t + 1) * P)
            for i in range(SLABS):
                nc.tensor.matmul(
                    out=sums[:, 1, t, :],
                    lhsT=live[("q", g * SLABS + i)][:, tile_tokens],
                    rhs=live[("k_sum_of_head", g * SLABS + i)][:, t // BATCH_TILES, :],
                    start=(i == 0),
                    stop=(i == SLABS - 1),
                )
            nc.tensor.matmul(
                out=sums[:, 0, t, :],
                lhsT=live[("product", g * SLABS)][:, tile_tokens],
                rhs=head_of_row[:],
                start=True,
                stop=True,
            )

        def divide(g):
            sums = live[("sums", g)]
            denominator = stage.tile([P, TILES, HEADS], F32)
            nc.vector.tensor_scalar(
                out=denominator[:], in0=sums[:, 1, :, 0:HEADS], scalar1=NORM_EPS, scalar2=None, op0=ALU.add
            )
            inverse = stage.tile([P, TILES, HEADS], F32)
            nc.vector.reciprocal(out=inverse[:], in_=denominator[:])
            ratio = stage.tile([P, TILES, HEADS], F32)
            nc.vector.tensor_tensor(
                out=ratio[:], in0=sums[:, 0, :, 0:HEADS], in1=inverse[:], op=ALU.mult
            )
            live[("ratio", g)] = ratio

        def value(w):
            g, t = divmod(w, TILES)
            b, j = divmod(t, BATCH_TILES)
            tile_tokens = slice(w * P, (w + 1) * P)
            if g < GROUPS - 1:
                v = aux_psum.tile([P, HIDDEN], F32, tag="aux")
            else:
                v = proj_psum.tile([P, HIDDEN], F32, tag="proj")
            nc.tensor.matmul_mx(
                out=v[:],
                lhsT=x_codes[:, tile_tokens].bitcast(FP8X4),
                lhsT_scale=x_scales[:, tile_tokens],
                rhs=wv_codes[:].bitcast(FP8X4),
                rhs_scale=wv_scales[:],
                start=True,
                stop=True,
            )
            if j == 0:
                z = work.tile([P, BATCH_TILES, HIDDEN], F32)
                live[("z", g, b)] = z
            z = live[("z", g, b)]
            nc.vector.tensor_tensor(
                out=z[:, j, :].rearrange("r (n d) -> r n d", n=HEADS),
                in0=v[:].rearrange("r (n d) -> r n d", n=HEADS),
                in1=live[("ratio", g)][:, t, :].unsqueeze(2).to_broadcast([P, HEADS, HEAD_DIM]),
                op=ALU.mult,
            )
            if j == BATCH_TILES - 1:
                nc.sync.dma_start(
                    out=out[GROUP_BATCHES * g + b].rearrange("(r j) f -> r (j f)", j=BATCH_TILES),
                    in_=z[:].rearrange("r j f -> r (j f)"),
                )

        transpose_x(0)
        quantise_slab(0)
        quantise_x(0)

        for s in range(UNITS + VALUE_LAG):
            if s < UNITS:
                project(s)
            if s + 1 < SLABS:
                quantise_slab(s + 1)
            if s >= VALUE_LAG:
                value(s - VALUE_LAG)
            if 0 <= s - SUMS_LAG < UNITS:
                head_sums(s - SUMS_LAG)
                if (s - SUMS_LAG) % TILES == TILES - 1:
                    divide((s - SUMS_LAG) // TILES)
            if s < UNITS and s % SLABS == 2:
                add_products(nc.gpsimd, s - 2, s - 1)
            last_unit = s - ADD_LAG
            group_is_multiplied = 0 <= last_unit < UNITS and last_unit % SLABS == SLABS - 1
            if group_is_multiplied:
                add_products(nc.vector, last_unit - 1, last_unit)
            if s < UNITS:
                combine(s)
            if group_is_multiplied:
                add_products(nc.vector, last_unit - 3, last_unit - 1)
            if s == SLABS - 1:
                regroup_wv()
            if s == SLABS:
                quantise(wv_grouped[:], wv_codes[:], wv_scales[:])
            if s // SLABS + 1 < GROUPS:
                if s % SLABS == 0:
                    transpose_x(s // SLABS + 1)
                if s % SLABS == 1:
                    quantise_x(s // SLABS + 1)
